import numpy as np
import ml_dtypes


def mxq(x, axis, fmt="e4m3"):
    dtype, down = {"e4m3": (ml_dtypes.float8_e4m3fn, 7), "e5m2": (ml_dtypes.float8_e5m2, 14)}[fmt]
    v = np.moveaxis(np.asarray(x, np.float32).astype(ml_dtypes.bfloat16).astype(np.float64), axis, -1)
    blocks = v.reshape(v.shape[:-1] + (-1, 32))
    amax = np.abs(blocks).max(-1, keepdims=True)
    byte = np.maximum(np.where(amax > 0, np.frexp(amax)[1] - 1 + 127, 0) - down, 1)
    scale = np.exp2(byte - 127.0)
    codes = (blocks / scale).astype(np.float32).astype(dtype).astype(np.float64)
    return np.moveaxis((codes * scale).reshape(v.shape), -1, axis)


WIDE = False


def mx_kscale(k):
    if not WIDE:
        return np.ones(k)
    levels = np.array([10, -10, 5, -5, 0])
    a = np.random.permutation(np.resize(levels, k // 512 * 4)).reshape(k // 512, 4)
    idx = np.arange(k)
    return np.exp2(a[idx // 512, idx % 128 // 32])


BF16 = ml_dtypes.bfloat16


def bf(x):
    return np.asarray(x, np.float32).astype(BF16)


def f64(x):
    return np.asarray(x).astype(np.float64)


B, S, D, H, QL, KL, ND, VD, RD = 4, 1024, 1024, 4, 512, 512, 64, 128, 64
QH = ND + RD
BASE = 10000.0


def rope(v):
    d = v.shape[-1]
    inv_freq = BASE ** (-np.arange(0, d, 2) / d)
    ang = np.arange(v.shape[1])[:, None] * inv_freq[None, :]
    cos = np.cos(ang)[None, :, None, :]
    sin = np.sin(ang)[None, :, None, :]
    v1 = v[..., 0::2]
    v2 = v[..., 1::2]
    o1 = v1 * cos - v2 * sin
    o2 = v1 * sin + v2 * cos
    return np.stack([o1, o2], axis=-1).reshape(v.shape)


def setup_inputs():
    s, t = mx_kscale(D), mx_kscale(QL)
    return {"x": bf(np.random.standard_normal((B, S, D)) * s),
            "Wqa": bf(np.random.standard_normal((D, QL)) / np.sqrt(D) / s[:, None] * t),
            "Wqb": bf(np.random.standard_normal((QL, H * QH)) / np.sqrt(QL) / t[:, None])}


def reference(x, Wqa, Wqb):
    cq = mxq(f64(x), 2, "e4m3") @ mxq(f64(Wqa), 0, "e4m3")
    q = (mxq(cq, 2, "e4m3") @ mxq(f64(Wqb), 0, "e4m3")).reshape(B, S, H, QH)
    q_nope, q_pe = q[..., :ND], q[..., ND:]
    return np.concatenate([q_nope, rope(q_pe)], axis=-1)

@@ -1,0 +1,274 @@
+import math
+from contextlib import ExitStack
+
+import concourse.masks as masks
+import concourse.mybir as mybir
+
+F32 = mybir.dt.float32
+BF16 = mybir.dt.bfloat16
+I32 = mybir.dt.int32
+U32 = mybir.dt.uint32
+U8 = mybir.dt.uint8
+FP8X4 = mybir.dt.float8_e4m3fn_x4
+ALU = mybir.AluOpType
+SIN = mybir.ActivationFunctionType.Sin
+
+P = 128
+PACK = 4
+K_PASS = P * PACK
+
+TOKENS = 4 * 1024
+SEQ = 1024
+D = 1024
+QL = 512
+HEADS = 4
+HEAD_DIM = 128
+PLAIN = 64
+PAIRS = 32
+BASE = 10000.0
+
+PASSES = D // K_PASS
+WORDS = D // 2
+TILES = 2
+UNIT = TILES * P
+UNITS = TOKENS // UNIT
+TABLES = SEQ // P
+HALF = HEADS * PLAIN
+
+FLOPS = 2 * TOKENS * D * QL + 2 * TOKENS * QL * HEADS * HEAD_DIM
+
+TWO_PI = 2.0 * math.pi
+TWO_PI_HI = 6.28125
+TWO_PI_LO = TWO_PI - TWO_PI_HI
+
+ROUND_FIRST = 1
+ROUND_CQ = 2
+ROUND_SECOND = 3
+ROUND_ROTATE = 4
+
+
+def build_rotation_tables(nc, pool, cos_sin, nsin_cos):
+    position_int = pool.tile([P, TABLES], I32)
+    nc.gpsimd.iota(
+        position_int[:], pattern=[[UNIT, TABLES // TILES], [1, TILES]], base=0, channel_multiplier=TILES
+    )
+    inv_freq = pool.tile([P, PAIRS], F32)
+    nc.gpsimd.memset(inv_freq[:, 0:1], 1.0)
+    for n in (1, 2, 4, 8, 16):
+        nc.gpsimd.tensor_scalar(
+            out=inv_freq[:, n : 2 * n],
+            in0=inv_freq[:, 0:n],
+            scalar1=BASE ** (-n / PAIRS),
+            scalar2=0.0,
+            op0=ALU.mult,
+            op1=ALU.add,
+        )
+    position = pool.tile([P, TABLES], F32)
+    nc.vector.tensor_copy(out=position[:], in_=position_int[:])
+    shape = [P, TABLES, PAIRS]
+    angle = pool.tile(shape, F32)
+    nc.vector.tensor_tensor(
+        out=angle[:],
+        in0=position[:].unsqueeze(2).to_broadcast(shape),
+        in1=inv_freq[:].unsqueeze(1).to_broadcast(shape),
+        op=ALU.mult,
+    )
+    turns_int = pool.tile(shape, I32)
+    nc.vector.tensor_scalar(out=turns_int[:], in0=angle[:], scalar1=1.0 / TWO_PI, scalar2=None, op0=ALU.mult)
+    turns = pool.tile(shape, F32)
+    nc.vector.tensor_copy(out=turns[:], in_=turns_int[:])
+    phase = pool.tile([P, 2, TABLES, PAIRS], F32)
+    nc.vector.scalar_tensor_tensor(
+        out=phase[:, 0], in0=turns[:], scalar=-TWO_PI_HI, in1=angle[:], op0=ALU.mult, op1=ALU.add
+    )
+    nc.vector.scalar_tensor_tensor(
+        out=phase[:, 0], in0=turns[:], scalar=-TWO_PI_LO, in1=phase[:, 0], op0=ALU.mult, op1=ALU.add
+    )
+    nc.vector.tensor_scalar(out=phase[:, 1], in0=phase[:, 0], scalar1=0.5 * math.pi, scalar2=None, op0=ALU.add)
+    turn = pool.tile([P, 2, TABLES, PAIRS], F32)
+    nc.vector.tensor_scalar(out=turn[:], in0=phase[:], scalar1=math.pi, scalar2=TWO_PI, op0=ALU.is_gt, op1=ALU.mult)
+    nc.vector.tensor_tensor(out=phase[:], in0=phase[:], in1=turn[:], op=ALU.subtract)
+    nc.vector.tensor_scalar(out=turn[:], in0=phase[:], scalar1=-math.pi, scalar2=TWO_PI, op0=ALU.is_lt, op1=ALU.mult)
+    nc.vector.tensor_tensor(out=phase[:], in0=phase[:], in1=turn[:], op=ALU.add)
+    nc.scalar.activation(out=cos_sin[:, :, :, 0], in_=phase[:, 1], func=SIN)
+    nc.scalar.activation(out=cos_sin[:, :, :, 1], in_=phase[:, 0], func=SIN)
+    nc.scalar.activation(out=nsin_cos[:, :, :, 0], in_=phase[:, 0], func=SIN, scale=-1.0)
+    nc.scalar.activation(out=nsin_cos[:, :, :, 1], in_=phase[:, 1], func=SIN)
+
+
+def tile_multilatentattention_pa_t_kernel(tc, x, Wqa, Wqb, out):
+    nc = tc.nc
+    x_units = x.flatten_outer_dims().rearrange("(n p t) k -> n p (t k)", p=P, t=TILES)
+    out_units = out.rearrange("b s h d -> (b s) (h d)").rearrange("(n p t) f -> n p (t f)", p=P, t=TILES)
+
+    with ExitStack() as ctx:
+        keep = ctx.enter_context(tc.tile_pool(name="keep", bufs=1))
+        x_pool = ctx.enter_context(tc.tile_pool(name="x_pool", bufs=UNITS))
+        stage = ctx.enter_context(tc.tile_pool(name="stage", bufs=3))
+        results = ctx.enter_context(tc.tile_pool(name="results", bufs=4))
+        psum = ctx.enter_context(tc.psum_pool(name="psum", bufs=2))
+        ctx.enter_context(tc.manual_schedule())
+
+        wa_raw = keep.tile([P, PASSES, PACK, QL], BF16)
+        nc.sync.dma_start(
+            out=wa_raw[:].rearrange("p g t c -> p (g t c)").rearrange("p (a c) -> p a c", a=2 * PASSES),
+            in_=Wqa.rearrange("(a p e) c -> p a (e c)", p=P, e=2),
+        )
+        wb_raw = keep.tile([P, PACK, HEADS * HEAD_DIM], BF16)
+        x_tiles = []
+        for n in range(UNITS):
+            x_sb = x_pool.tile([P, TILES * D], BF16)
+            nc.sync.dma_start(out=x_sb[:], in_=x_units[n])
+            x_tiles.append(x_sb)
+            if n == 0:
+                nc.sync.dma_start(
+                    out=wb_raw[:].rearrange("p j f -> p (j f)"), in_=Wqb.rearrange("(p j) f -> p (j f)", j=PACK)
+                )
+
+        cos_sin = keep.tile([P, TABLES, PAIRS, 2], F32)
+        nsin_cos = keep.tile([P, TABLES, PAIRS, 2], F32)
+        build_rotation_tables(nc, keep, cos_sin, nsin_cos)
+        identity = keep.tile([P, P], F32)
+        masks.make_identity(nc, identity[:])
+
+        wa_grouped = keep.tile([P, PASSES, QL * PACK], BF16, align_bytes=64)
+        wa_codes = keep.tile([P, PASSES, QL], U32, align_bytes=64)
+        wa_scales = keep.tile([P, PASSES, QL], U8, align_bytes=64)
+        for g in range(PASSES):
+            nc.vector.tensor_copy(
+                out=wa_grouped[:, g].rearrange("p (m i t) -> p m i t", m=PACK, t=PACK),
+                in_=wa_raw[:, g].rearrange("p t (i m) -> p m i t", m=PACK),
+            )
+        for g in range(PASSES):
+            nc.vector.quantize_mx(out=wa_codes[:, g].bitcast(FP8X4), scales=wa_scales[:, g], in_=wa_grouped[:, g])
+
+        wb_codes = keep.tile([P, 2 * HALF], U32, align_bytes=64)
+        wb_scales = keep.tile([P, 2 * HALF], U8, align_bytes=64)
+
+        def quantise_wqb():
+            wb_grouped = keep.tile([P, 2, HALF * PACK], BF16, align_bytes=64)
+            sorted_raw = wb_raw[:].rearrange("p j (h s f) -> p s h f j", s=2, f=PLAIN)
+            for s in range(2):
+                nc.vector.tensor_copy(
+                    out=wb_grouped[:, s].rearrange("p (h f j) -> p h f j", h=HEADS, j=PACK), in_=sorted_raw[:, s]
+                )
+            nc.vector.quantize_mx(
+                out=wb_codes[:].bitcast(FP8X4), scales=wb_scales[:], in_=wb_grouped[:].rearrange("p s c -> p (s c)")
+            )
+
+        x_grouped, x_packed, cq_grouped, cq_packed, rotated_banks, result_tiles = {}, {}, {}, {}, {}, {}
+
+        def transpose_x(n):
+            x_words = x_tiles[n][:].bitcast(F32)
+            grouped = stage.tile([P, PASSES * TILES * P * PACK], BF16, align_bytes=64, name="x_grouped")
+            grouped_words = grouped[:].bitcast(F32).rearrange("p (g t r u) -> p g t r u", g=PASSES, t=TILES, u=2)
+            for t in range(TILES):
+                x_t = psum.tile([P, 2 * PASSES, P], F32, name="x_t")
+                for a in range(2 * PASSES):
+                    first_word = t * WORDS + a * P
+                    nc.tensor.transpose(x_t[:, a, :], x_words[:, first_word : first_word + P], identity[:])
+                nc.scalar.copy(out=grouped_words[:, :, t], in_=x_t[:].rearrange("p (g u) r -> p g r u", u=2))
+            x_grouped[n] = grouped
+
+        def quantise_x(n):
+            codes = stage.tile([P, PASSES, TILES, P], U32, align_bytes=64, name="x_codes")
+            scales = stage.tile([P, PASSES, TILES, P], U8, align_bytes=64, name="x_scales")
+            nc.vector.quantize_mx(
+                out=codes[:].rearrange("p g t r -> p (g t r)").bitcast(FP8X4),
+                scales=scales[:].rearrange("p g t r -> p (g t r)"),
+                in_=x_grouped[n][:],
+            )
+            x_packed[n] = (codes, scales)
+
+        def first_product(n):
+            codes, scales = x_packed[n]
+            grouped = stage.tile([P, TILES, P, PACK], BF16, align_bytes=64, name="cq_grouped")
+            for t in range(TILES):
+                cq_t = psum.tile([P, PACK, P], F32, name="cq_t")
+                for m in range(PACK):
+                    columns = slice(m * P, (m + 1) * P)
+                    for g in range(PASSES):
+                        nc.tensor.matmul_mx(
+                            out=cq_t[:, m, :],
+                            lhsT=wa_codes[:, g, columns].bitcast(FP8X4),
+                            lhsT_scale=wa_scales[:, g, columns],
+                            rhs=codes[:, g, t, :].bitcast(FP8X4),
+                            rhs_scale=scales[:, g, t, :],
+                            start=(g == 0),
+                            stop=(g == PASSES - 1),
+                        )
+                nc.scalar.copy(out=grouped[:, t], in_=cq_t[:].rearrange("p m r -> p r m"))
+            cq_grouped[n] = grouped
+
+        def quantise_cq(n):
+            codes = stage.tile([P, TILES, P], U32, align_bytes=64, name="cq_codes")
+            scales = stage.tile([P, TILES, P], U8, align_bytes=64, name="cq_scales")
+            nc.vector.quantize_mx(
+                out=codes[:].rearrange("p t r -> p (t r)").bitcast(FP8X4),
+                scales=scales[:].rearrange("p t r -> p (t r)"),
+                in_=cq_grouped[n][:].rearrange("p t r m -> p (t r m)"),
+            )
+            cq_packed[n] = (codes, scales)
+
+        def second_product(n):
+            codes, scales = cq_packed[n]
+            plain_bank = psum.tile([P, TILES, HALF], F32, name="plain_bank")
+            rotated_bank = psum.tile([P, TILES, HALF], F32, name="rotated_bank")
+            for t in range(TILES):
+                for s, bank in enumerate((plain_bank, rotated_bank)):
+                    columns = slice(s * HALF, (s + 1) * HALF)
+                    nc.tensor.matmul_mx(
+                        out=bank[:, t, :],
+                        lhsT=codes[:, t, :].bitcast(FP8X4),
+                        lhsT_scale=scales[:, t, :],
+                        rhs=wb_codes[:, columns].bitcast(FP8X4),
+                        rhs_scale=wb_scales[:, columns],
+                        start=True,
+                        stop=True,
+                    )
+            result = results.tile([P, TILES, HEADS, HEAD_DIM], F32, name="result")
+            nc.scalar.copy(out=result[:, :, :, 0:PLAIN], in_=plain_bank[:].rearrange("p t (h f) -> p t h f", f=PLAIN))
+            rotated_banks[n] = rotated_bank
+            result_tiles[n] = result
+
+        def rotate_and_store(n):
+            shape = [P, TILES, HEADS, PAIRS, 2]
+            pairs = rotated_banks[n][:].rearrange("p t (h j e) -> p t h j e", h=HEADS, e=2)
+            first_table = (n % (TABLES // TILES)) * TILES
+            tables = slice(first_table, first_table + TILES)
+            result = result_tiles[n]
+            rotated = result[:, :, :, PLAIN:HEAD_DIM].rearrange("p t h (j e) -> p t h j e", e=2)
+            from_w = stage.tile(shape, F32, name="from_w")
+            nc.vector.tensor_tensor(
+                out=rotated,
+                in0=pairs[:, :, :, :, 0:1].to_broadcast(shape),
+                in1=cos_sin[:, tables].unsqueeze(2).to_broadcast(shape),
+                op=ALU.mult,
+            )
+            nc.vector.tensor_tensor(
+                out=from_w[:],
+                in0=pairs[:, :, :, :, 1:2].to_broadcast(shape),
+                in1=nsin_cos[:, tables].unsqueeze(2).to_broadcast(shape),
+                op=ALU.mult,
+            )
+            nc.vector.tensor_tensor(out=rotated, in0=rotated, in1=from_w[:], op=ALU.add)
+            nc.sync.dma_start(out=out_units[n], in_=result[:].rearrange("p t h d -> p (t h d)"))
+
+        def in_range(n):
+            return 0 <= n < UNITS
+
+        for i in range(UNITS + ROUND_ROTATE):
+            if in_range(i):
+                transpose_x(i)
+            if in_range(i - ROUND_FIRST):
+                first_product(i - ROUND_FIRST)
+            if in_range(i - ROUND_SECOND):
+                second_product(i - ROUND_SECOND)
+            if in_range(i - ROUND_ROTATE):
+                rotate_and_store(i - ROUND_ROTATE)
+            if in_range(i - ROUND_CQ):
+                quantise_cq(i - ROUND_CQ)
+            if in_range(i):
+                quantise_x(i)
+            if i == 0:
+                quantise_wqb()

@@ -38,13 +38,12 @@ HALF = HEADS * PLAIN
 FLOPS = 2 * TOKENS * D * QL + 2 * TOKENS * QL * HEADS * HEAD_DIM
 
 TWO_PI = 2.0 * math.pi
-TWO_PI_HI = 6.28125
-TWO_PI_LO = TWO_PI - TWO_PI_HI
 
 ROUND_FIRST = 1
-ROUND_CQ = 2
-ROUND_SECOND = 3
-ROUND_ROTATE = 4
+ROUND_SECOND = 2
+ROUND_ROTATE = 3
+
+WQA_VECTOR_COLUMNS = 96
 
 
 def build_rotation_tables(nc, pool, cos_sin, nsin_cos):
@@ -53,47 +52,42 @@ def build_rotation_tables(nc, pool, cos_sin, nsin_cos):
         position_int[:], pattern=[[UNIT, TABLES // TILES], [1, TILES]], base=0, channel_multiplier=TILES
     )
     inv_freq = pool.tile([P, PAIRS], F32)
-    nc.gpsimd.memset(inv_freq[:, 0:1], 1.0)
+    nc.vector.memset(inv_freq[:, 0:1], 1.0)
     for n in (1, 2, 4, 8, 16):
-        nc.gpsimd.tensor_scalar(
-            out=inv_freq[:, n : 2 * n],
-            in0=inv_freq[:, 0:n],
-            scalar1=BASE ** (-n / PAIRS),
-            scalar2=0.0,
-            op0=ALU.mult,
-            op1=ALU.add,
+        nc.vector.tensor_scalar(
+            out=inv_freq[:, n : 2 * n], in0=inv_freq[:, 0:n], scalar1=BASE ** (-n / PAIRS), scalar2=None, op0=ALU.mult
         )
     position = pool.tile([P, TABLES], F32)
-    nc.vector.tensor_copy(out=position[:], in_=position_int[:])
+    nc.vector.tensor_scalar(out=position[:], in0=position_int[:], scalar1=1.0 / TWO_PI, scalar2=None, op0=ALU.mult)
     shape = [P, TABLES, PAIRS]
-    angle = pool.tile(shape, F32)
+    turns = pool.tile(shape, F32)
     nc.vector.tensor_tensor(
-        out=angle[:],
+        out=turns[:],
         in0=position[:].unsqueeze(2).to_broadcast(shape),
         in1=inv_freq[:].unsqueeze(1).to_broadcast(shape),
         op=ALU.mult,
     )
-    turns_int = pool.tile(shape, I32)
-    nc.vector.tensor_scalar(out=turns_int[:], in0=angle[:], scalar1=1.0 / TWO_PI, scalar2=None, op0=ALU.mult)
-    turns = pool.tile(shape, F32)
-    nc.vector.tensor_copy(out=turns[:], in_=turns_int[:])
-    phase = pool.tile([P, 2, TABLES, PAIRS], F32)
+    whole_int = pool.tile(shape, I32)
+    nc.vector.tensor_copy(out=whole_int[:], in_=turns[:])
+    whole = pool.tile(shape, F32)
+    nc.vector.tensor_copy(out=whole[:], in_=whole_int[:])
+    part = pool.tile(shape, F32)
+    nc.vector.tensor_tensor(out=part[:], in0=turns[:], in1=whole[:], op=ALU.subtract)
+    phase = pool.tile([P, TABLES, PAIRS, 2], F32)
+    over = pool.tile(shape, F32)
+    nc.vector.tensor_scalar(out=over[:], in0=part[:], scalar1=0.5, scalar2=None, op0=ALU.is_gt)
+    nc.vector.tensor_tensor(out=phase[:, :, :, 1], in0=part[:], in1=over[:], op=ALU.subtract)
+    nc.vector.tensor_scalar(out=over[:], in0=phase[:, :, :, 1], scalar1=0.25, scalar2=None, op0=ALU.is_gt)
     nc.vector.scalar_tensor_tensor(
-        out=phase[:, 0], in0=turns[:], scalar=-TWO_PI_HI, in1=angle[:], op0=ALU.mult, op1=ALU.add
+        out=phase[:, :, :, 0], in0=phase[:, :, :, 1], scalar=0.25, in1=over[:], op0=ALU.add, op1=ALU.subtract
     )
-    nc.vector.scalar_tensor_tensor(
-        out=phase[:, 0], in0=turns[:], scalar=-TWO_PI_LO, in1=phase[:, 0], op0=ALU.mult, op1=ALU.add
+    nc.scalar.activation(out=cos_sin[:], in_=phase[:], func=SIN, scale=TWO_PI)
+    nc.gpsimd.tensor_scalar(
+        out=nsin_cos[:, :, :, 0], in0=cos_sin[:, :, :, 1], scalar1=-1.0, scalar2=0.0, op0=ALU.mult, op1=ALU.add
     )
-    nc.vector.tensor_scalar(out=phase[:, 1], in0=phase[:, 0], scalar1=0.5 * math.pi, scalar2=None, op0=ALU.add)
-    turn = pool.tile([P, 2, TABLES, PAIRS], F32)
-    nc.vector.tensor_scalar(out=turn[:], in0=phase[:], scalar1=math.pi, scalar2=TWO_PI, op0=ALU.is_gt, op1=ALU.mult)
-    nc.vector.tensor_tensor(out=phase[:], in0=phase[:], in1=turn[:], op=ALU.subtract)
-    nc.vector.tensor_scalar(out=turn[:], in0=phase[:], scalar1=-math.pi, scalar2=TWO_PI, op0=ALU.is_lt, op1=ALU.mult)
-    nc.vector.tensor_tensor(out=phase[:], in0=phase[:], in1=turn[:], op=ALU.add)
-    nc.scalar.activation(out=cos_sin[:, :, :, 0], in_=phase[:, 1], func=SIN)
-    nc.scalar.activation(out=cos_sin[:, :, :, 1], in_=phase[:, 0], func=SIN)
-    nc.scalar.activation(out=nsin_cos[:, :, :, 0], in_=phase[:, 0], func=SIN, scale=-1.0)
-    nc.scalar.activation(out=nsin_cos[:, :, :, 1], in_=phase[:, 1], func=SIN)
+    nc.gpsimd.tensor_scalar(
+        out=nsin_cos[:, :, :, 1], in0=cos_sin[:, :, :, 0], scalar1=1.0, scalar2=0.0, op0=ALU.mult, op1=ALU.add
+    )
 
 
 def tile_multilatentattention_pa_t_kernel(tc, x, Wqa, Wqb, out):
@@ -135,10 +129,10 @@ def tile_multilatentattention_pa_t_kernel(tc, x, Wqa, Wqb, out):
         wa_codes = keep.tile([P, PASSES, QL], U32, align_bytes=64)
         wa_scales = keep.tile([P, PASSES, QL], U8, align_bytes=64)
         for g in range(PASSES):
-            nc.vector.tensor_copy(
-                out=wa_grouped[:, g].rearrange("p (m i t) -> p m i t", m=PACK, t=PACK),
-                in_=wa_raw[:, g].rearrange("p t (i m) -> p m i t", m=PACK),
-            )
+            grouped = wa_grouped[:, g].rearrange("p (m i t) -> p m i t", m=PACK, t=PACK)
+            raw = wa_raw[:, g].rearrange("p t (i m) -> p m i t", m=PACK)
+            nc.vector.tensor_copy(out=grouped[:, :, 0:WQA_VECTOR_COLUMNS], in_=raw[:, :, 0:WQA_VECTOR_COLUMNS])
+            nc.scalar.copy(out=grouped[:, :, WQA_VECTOR_COLUMNS:P], in_=raw[:, :, WQA_VECTOR_COLUMNS:P])
         for g in range(PASSES):
             nc.vector.quantize_mx(out=wa_codes[:, g].bitcast(FP8X4), scales=wa_scales[:, g], in_=wa_grouped[:, g])
 
@@ -263,11 +257,10 @@ def tile_multilatentattention_pa_t_kernel(tc, x, Wqa, Wqb, out):
             if in_range(i - ROUND_FIRST):
                 first_product(i - ROUND_FIRST)
             if in_range(i - ROUND_SECOND):
+                quantise_cq(i - ROUND_SECOND)
                 second_product(i - ROUND_SECOND)
             if in_range(i - ROUND_ROTATE):
                 rotate_and_store(i - ROUND_ROTATE)
-            if in_range(i - ROUND_CQ):
-                quantise_cq(i - ROUND_CQ)
             if in_range(i):
                 quantise_x(i)
             if i == 0:

@@ -46,11 +46,7 @@ ROUND_ROTATE = 3
 WQA_VECTOR_COLUMNS = 96
 
 
-def build_rotation_tables(nc, pool, cos_sin, nsin_cos):
-    position_int = pool.tile([P, TABLES], I32)
-    nc.gpsimd.iota(
-        position_int[:], pattern=[[UNIT, TABLES // TILES], [1, TILES]], base=0, channel_multiplier=TILES
-    )
+def build_rotation_tables(nc, pool, position_int, cos_sin, nsin_cos):
     inv_freq = pool.tile([P, PAIRS], F32)
     nc.vector.memset(inv_freq[:, 0:1], 1.0)
     for n in (1, 2, 4, 8, 16):
@@ -119,11 +115,15 @@ def tile_multilatentattention_pa_t_kernel(tc, x, Wqa, Wqb, out):
                     out=wb_raw[:].rearrange("p j f -> p (j f)"), in_=Wqb.rearrange("(p j) f -> p (j f)", j=PACK)
                 )
 
-        cos_sin = keep.tile([P, TABLES, PAIRS, 2], F32)
-        nsin_cos = keep.tile([P, TABLES, PAIRS, 2], F32)
-        build_rotation_tables(nc, keep, cos_sin, nsin_cos)
+        position_int = keep.tile([P, TABLES], I32)
+        nc.gpsimd.iota(
+            position_int[:], pattern=[[UNIT, TABLES // TILES], [1, TILES]], base=0, channel_multiplier=TILES
+        )
         identity = keep.tile([P, P], F32)
         masks.make_identity(nc, identity[:])
+        cos_sin = keep.tile([P, TABLES, PAIRS, 2], F32)
+        nsin_cos = keep.tile([P, TABLES, PAIRS, 2], F32)
+        build_rotation_tables(nc, keep, position_int, cos_sin, nsin_cos)
 
         wa_grouped = keep.tile([P, PASSES, QL * PACK], BF16, align_bytes=64)
         wa_codes = keep.tile([P, PASSES, QL], U32, align_bytes=64)
@@ -150,7 +150,7 @@ def tile_multilatentattention_pa_t_kernel(tc, x, Wqa, Wqb, out):
                 out=wb_codes[:].bitcast(FP8X4), scales=wb_scales[:], in_=wb_grouped[:].rearrange("p s c -> p (s c)")
             )
 
-        x_grouped, x_packed, cq_grouped, cq_packed, rotated_banks, result_tiles = {}, {}, {}, {}, {}, {}
+        x_grouped, x_packed, cq_grouped, cq_packed, rotated_banks, result_tiles, w_products = {}, {}, {}, {}, {}, {}, {}
 
         def transpose_x(n):
             x_words = x_tiles[n][:].bitcast(F32)
@@ -225,16 +225,17 @@ def tile_multilatentattention_pa_t_kernel(tc, x, Wqa, Wqb, out):
             rotated_banks[n] = rotated_bank
             result_tiles[n] = result
 
-        def rotate_and_store(n):
+        def rotated_part(n):
+            return result_tiles[n][:, :, :, PLAIN:HEAD_DIM].rearrange("p t h (j e) -> p t h j e", e=2)
+
+        def rotation_products(n):
             shape = [P, TILES, HEADS, PAIRS, 2]
             pairs = rotated_banks[n][:].rearrange("p t (h j e) -> p t h j e", h=HEADS, e=2)
             first_table = (n % (TABLES // TILES)) * TILES
             tables = slice(first_table, first_table + TILES)
-            result = result_tiles[n]
-            rotated = result[:, :, :, PLAIN:HEAD_DIM].rearrange("p t h (j e) -> p t h j e", e=2)
             from_w = stage.tile(shape, F32, name="from_w")
             nc.vector.tensor_tensor(
-                out=rotated,
+                out=rotated_part(n),
                 in0=pairs[:, :, :, :, 0:1].to_broadcast(shape),
                 in1=cos_sin[:, tables].unsqueeze(2).to_broadcast(shape),
                 op=ALU.mult,
@@ -245,8 +246,11 @@ def tile_multilatentattention_pa_t_kernel(tc, x, Wqa, Wqb, out):
                 in1=nsin_cos[:, tables].unsqueeze(2).to_broadcast(shape),
                 op=ALU.mult,
             )
-            nc.vector.tensor_tensor(out=rotated, in0=rotated, in1=from_w[:], op=ALU.add)
-            nc.sync.dma_start(out=out_units[n], in_=result[:].rearrange("p t h d -> p (t h d)"))
+            w_products[n] = from_w
+
+        def add_and_store(n):
+            nc.vector.tensor_tensor(out=rotated_part(n), in0=rotated_part(n), in1=w_products[n][:], op=ALU.add)
+            nc.sync.dma_start(out=out_units[n], in_=result_tiles[n][:].rearrange("p t h d -> p (t h d)"))
 
         def in_range(n):
             return 0 <= n < UNITS
@@ -260,8 +264,10 @@ def tile_multilatentattention_pa_t_kernel(tc, x, Wqa, Wqb, out):
                 quantise_cq(i - ROUND_SECOND)
                 second_product(i - ROUND_SECOND)
             if in_range(i - ROUND_ROTATE):
-                rotate_and_store(i - ROUND_ROTATE)
+                rotation_products(i - ROUND_ROTATE)
             if in_range(i):
                 quantise_x(i)
+            if in_range(i - ROUND_ROTATE):
+                add_and_store(i - ROUND_ROTATE)
             if i == 0:
                 quantise_wqb()

@@ -39,51 +39,35 @@ FLOPS = 2 * TOKENS * D * QL + 2 * TOKENS * QL * HEADS * HEAD_DIM
 
 TWO_PI = 2.0 * math.pi
 
-ROUND_FIRST = 1
-ROUND_SECOND = 2
-ROUND_ROTATE = 3
+ROUND_FIRST = 2
+ROUND_SECOND = 3
+ROUND_ROTATE = 4
 
 WQA_VECTOR_COLUMNS = 96
 
 
-def build_rotation_tables(nc, pool, position_int, cos_sin, nsin_cos):
-    inv_freq = pool.tile([P, PAIRS], F32)
-    nc.vector.memset(inv_freq[:, 0:1], 1.0)
+def rotation_phases(nc, pool, position_int):
+    shape = [P, TABLES, PAIRS, 2]
+    turns = pool.tile(shape, F32)
+    nc.vector.tensor_scalar(
+        out=turns[:, :, 0:1, 1], in0=position_int[:].unsqueeze(2), scalar1=1.0 / TWO_PI, scalar2=None, op0=ALU.mult
+    )
     for n in (1, 2, 4, 8, 16):
         nc.vector.tensor_scalar(
-            out=inv_freq[:, n : 2 * n], in0=inv_freq[:, 0:n], scalar1=BASE ** (-n / PAIRS), scalar2=None, op0=ALU.mult
+            out=turns[:, :, n : 2 * n, 1],
+            in0=turns[:, :, 0:n, 1],
+            scalar1=BASE ** (-n / PAIRS),
+            scalar2=None,
+            op0=ALU.mult,
         )
-    position = pool.tile([P, TABLES], F32)
-    nc.vector.tensor_scalar(out=position[:], in0=position_int[:], scalar1=1.0 / TWO_PI, scalar2=None, op0=ALU.mult)
-    shape = [P, TABLES, PAIRS]
-    turns = pool.tile(shape, F32)
-    nc.vector.tensor_tensor(
-        out=turns[:],
-        in0=position[:].unsqueeze(2).to_broadcast(shape),
-        in1=inv_freq[:].unsqueeze(1).to_broadcast(shape),
-        op=ALU.mult,
-    )
+    nc.vector.tensor_scalar(out=turns[:, :, :, 0], in0=turns[:, :, :, 1], scalar1=0.25, scalar2=None, op0=ALU.add)
     whole_int = pool.tile(shape, I32)
     nc.vector.tensor_copy(out=whole_int[:], in_=turns[:])
     whole = pool.tile(shape, F32)
     nc.vector.tensor_copy(out=whole[:], in_=whole_int[:])
-    part = pool.tile(shape, F32)
-    nc.vector.tensor_tensor(out=part[:], in0=turns[:], in1=whole[:], op=ALU.subtract)
-    phase = pool.tile([P, TABLES, PAIRS, 2], F32)
-    over = pool.tile(shape, F32)
-    nc.vector.tensor_scalar(out=over[:], in0=part[:], scalar1=0.5, scalar2=None, op0=ALU.is_gt)
-    nc.vector.tensor_tensor(out=phase[:, :, :, 1], in0=part[:], in1=over[:], op=ALU.subtract)
-    nc.vector.tensor_scalar(out=over[:], in0=phase[:, :, :, 1], scalar1=0.25, scalar2=None, op0=ALU.is_gt)
-    nc.vector.scalar_tensor_tensor(
-        out=phase[:, :, :, 0], in0=phase[:, :, :, 1], scalar=0.25, in1=over[:], op0=ALU.add, op1=ALU.subtract
-    )
-    nc.scalar.activation(out=cos_sin[:], in_=phase[:], func=SIN, scale=TWO_PI)
-    nc.gpsimd.tensor_scalar(
-        out=nsin_cos[:, :, :, 0], in0=cos_sin[:, :, :, 1], scalar1=-1.0, scalar2=0.0, op0=ALU.mult, op1=ALU.add
-    )
-    nc.gpsimd.tensor_scalar(
-        out=nsin_cos[:, :, :, 1], in0=cos_sin[:, :, :, 0], scalar1=1.0, scalar2=0.0, op0=ALU.mult, op1=ALU.add
-    )
+    phase = pool.tile(shape, F32)
+    nc.vector.tensor_tensor(out=phase[:], in0=turns[:], in1=whole[:], op=ALU.subtract)
+    return phase
 
 
 def tile_multilatentattention_pa_t_kernel(tc, x, Wqa, Wqb, out):
@@ -121,36 +105,40 @@ def tile_multilatentattention_pa_t_kernel(tc, x, Wqa, Wqb, out):
         )
         identity = keep.tile([P, P], F32)
         masks.make_identity(nc, identity[:])
-        cos_sin = keep.tile([P, TABLES, PAIRS, 2], F32)
-        nsin_cos = keep.tile([P, TABLES, PAIRS, 2], F32)
-        build_rotation_tables(nc, keep, position_int, cos_sin, nsin_cos)
+        phase = rotation_phases(nc, keep, position_int)
 
         wa_grouped = keep.tile([P, PASSES, QL * PACK], BF16, align_bytes=64)
         wa_codes = keep.tile([P, PASSES, QL], U32, align_bytes=64)
         wa_scales = keep.tile([P, PASSES, QL], U8, align_bytes=64)
         for g in range(PASSES):
-            grouped = wa_grouped[:, g].rearrange("p (m i t) -> p m i t", m=PACK, t=PACK)
-            raw = wa_raw[:, g].rearrange("p t (i m) -> p m i t", m=PACK)
-            nc.vector.tensor_copy(out=grouped[:, :, 0:WQA_VECTOR_COLUMNS], in_=raw[:, :, 0:WQA_VECTOR_COLUMNS])
-            nc.scalar.copy(out=grouped[:, :, WQA_VECTOR_COLUMNS:P], in_=raw[:, :, WQA_VECTOR_COLUMNS:P])
+            wa_sorted = wa_grouped[:, g].rearrange("p (m i t) -> p m i t", m=PACK, t=PACK)
+            wa_rows = wa_raw[:, g].rearrange("p t (i m) -> p m i t", m=PACK)
+            nc.vector.tensor_copy(out=wa_sorted[:, :, 0:WQA_VECTOR_COLUMNS], in_=wa_rows[:, :, 0:WQA_VECTOR_COLUMNS])
+            nc.scalar.copy(out=wa_sorted[:, :, WQA_VECTOR_COLUMNS:P], in_=wa_rows[:, :, WQA_VECTOR_COLUMNS:P])
         for g in range(PASSES):
             nc.vector.quantize_mx(out=wa_codes[:, g].bitcast(FP8X4), scales=wa_scales[:, g], in_=wa_grouped[:, g])
 
+        cos_sin = keep.tile([P, TABLES, PAIRS, 2], F32)
+        nc.scalar.activation(out=cos_sin[:], in_=phase[:], func=SIN, scale=TWO_PI)
+        nsin_cos = keep.tile([P, TABLES, PAIRS, 2], F32)
         wb_codes = keep.tile([P, 2 * HALF], U32, align_bytes=64)
         wb_scales = keep.tile([P, 2 * HALF], U8, align_bytes=64)
 
-        def quantise_wqb():
+        def late_setup():
+            nc.scalar.mul(out=nsin_cos[:, :, :, 0], in_=cos_sin[:, :, :, 1], mul=-1.0)
+            nc.scalar.copy(out=nsin_cos[:, :, :, 1], in_=cos_sin[:, :, :, 0])
             wb_grouped = keep.tile([P, 2, HALF * PACK], BF16, align_bytes=64)
-            sorted_raw = wb_raw[:].rearrange("p j (h s f) -> p s h f j", s=2, f=PLAIN)
+            wb_sorted = wb_raw[:].rearrange("p j (h s f) -> p s h f j", s=2, f=PLAIN)
             for s in range(2):
                 nc.vector.tensor_copy(
-                    out=wb_grouped[:, s].rearrange("p (h f j) -> p h f j", h=HEADS, j=PACK), in_=sorted_raw[:, s]
+                    out=wb_grouped[:, s].rearrange("p (h f j) -> p h f j", h=HEADS, j=PACK), in_=wb_sorted[:, s]
                 )
             nc.vector.quantize_mx(
                 out=wb_codes[:].bitcast(FP8X4), scales=wb_scales[:], in_=wb_grouped[:].rearrange("p s c -> p (s c)")
             )
 
-        x_grouped, x_packed, cq_grouped, cq_packed, rotated_banks, result_tiles, w_products = {}, {}, {}, {}, {}, {}, {}
+        x_grouped, x_packed, cq_grouped, cq_packed = {}, {}, {}, {}
+        plain_banks, rotated_banks, result_tiles, w_products = {}, {}, {}, {}
 
         def transpose_x(n):
             x_words = x_tiles[n][:].bitcast(F32)
@@ -220,15 +208,19 @@ def tile_multilatentattention_pa_t_kernel(tc, x, Wqa, Wqb, out):
                         start=True,
                         stop=True,
                     )
-            result = results.tile([P, TILES, HEADS, HEAD_DIM], F32, name="result")
-            nc.scalar.copy(out=result[:, :, :, 0:PLAIN], in_=plain_bank[:].rearrange("p t (h f) -> p t h f", f=PLAIN))
+            plain_banks[n] = plain_bank
             rotated_banks[n] = rotated_bank
-            result_tiles[n] = result
+            result_tiles[n] = results.tile([P, TILES, HEADS, HEAD_DIM], F32, name="result")
+
+        def copy_plain(n, engine_copy):
+            engine_copy(
+                out=result_tiles[n][:, :, :, 0:PLAIN], in_=plain_banks[n][:].rearrange("p t (h f) -> p t h f", f=PLAIN)
+            )
 
         def rotated_part(n):
             return result_tiles[n][:, :, :, PLAIN:HEAD_DIM].rearrange("p t h (j e) -> p t h j e", e=2)
 
-        def rotation_products(n):
+        def rotate_and_store(n):
             shape = [P, TILES, HEADS, PAIRS, 2]
             pairs = rotated_banks[n][:].rearrange("p t (h j e) -> p t h j e", h=HEADS, e=2)
             first_table = (n % (TABLES // TILES)) * TILES
@@ -246,10 +238,7 @@ def tile_multilatentattention_pa_t_kernel(tc, x, Wqa, Wqb, out):
                 in1=nsin_cos[:, tables].unsqueeze(2).to_broadcast(shape),
                 op=ALU.mult,
             )
-            w_products[n] = from_w
-
-        def add_and_store(n):
-            nc.vector.tensor_tensor(out=rotated_part(n), in0=rotated_part(n), in1=w_products[n][:], op=ALU.add)
+            nc.gpsimd.tensor_tensor(out=rotated_part(n), in0=rotated_part(n), in1=from_w[:], op=ALU.add)
             nc.sync.dma_start(out=out_units[n], in_=result_tiles[n][:].rearrange("p t h d -> p (t h d)"))
 
         def in_range(n):
@@ -261,13 +250,16 @@ def tile_multilatentattention_pa_t_kernel(tc, x, Wqa, Wqb, out):
             if in_range(i - ROUND_FIRST):
                 first_product(i - ROUND_FIRST)
             if in_range(i - ROUND_SECOND):
-                quantise_cq(i - ROUND_SECOND)
                 second_product(i - ROUND_SECOND)
+                if (i - ROUND_SECOND) % 2 == 0:
+                    copy_plain(i - ROUND_SECOND, nc.scalar.copy)
             if in_range(i - ROUND_ROTATE):
-                rotation_products(i - ROUND_ROTATE)
+                if (i - ROUND_ROTATE) % 2 == 1:
+                    copy_plain(i - ROUND_ROTATE, nc.vector.tensor_copy)
+                rotate_and_store(i - ROUND_ROTATE)
             if in_range(i):
                 quantise_x(i)
-            if in_range(i - ROUND_ROTATE):
-                add_and_store(i - ROUND_ROTATE)
+            if in_range(i - ROUND_FIRST):
+                quantise_cq(i - ROUND_FIRST)
             if i == 0:
-                quantise_wqb()
+                late_setup()

@@ -42,6 +42,7 @@ TWO_PI = 2.0 * math.pi
 ROUND_FIRST = 2
 ROUND_SECOND = 3
 ROUND_ROTATE = 4
+ROUND_LATE_SETUP = 1
 
 WQA_VECTOR_COLUMNS = 96
 
@@ -73,7 +74,7 @@ def rotation_phases(nc, pool, position_int):
 def tile_multilatentattention_pa_t_kernel(tc, x, Wqa, Wqb, out):
     nc = tc.nc
     x_units = x.flatten_outer_dims().rearrange("(n p t) k -> n p (t k)", p=P, t=TILES)
-    out_units = out.rearrange("b s h d -> (b s) (h d)").rearrange("(n p t) f -> n p (t f)", p=P, t=TILES)
+    out_units = out.rearrange("b s h d -> (b s) (h d)").rearrange("(n p t) f -> n p t f", p=P, t=TILES)
 
     with ExitStack() as ctx:
         keep = ctx.enter_context(tc.tile_pool(name="keep", bufs=1))
@@ -94,7 +95,7 @@ def tile_multilatentattention_pa_t_kernel(tc, x, Wqa, Wqb, out):
             x_sb = x_pool.tile([P, TILES * D], BF16)
             nc.sync.dma_start(out=x_sb[:], in_=x_units[n])
             x_tiles.append(x_sb)
-            if n == 0:
+            if n == ROUND_FIRST:
                 nc.sync.dma_start(
                     out=wb_raw[:].rearrange("p j f -> p (j f)"), in_=Wqb.rearrange("(p j) f -> p (j f)", j=PACK)
                 )
@@ -138,7 +139,7 @@ def tile_multilatentattention_pa_t_kernel(tc, x, Wqa, Wqb, out):
             )
 
         x_grouped, x_packed, cq_grouped, cq_packed = {}, {}, {}, {}
-        plain_banks, rotated_banks, result_tiles, w_products = {}, {}, {}, {}
+        plain_banks, rotated_banks, result_tiles = {}, {}, {}
 
         def transpose_x(n):
             x_words = x_tiles[n][:].bitcast(F32)
@@ -217,29 +218,34 @@ def tile_multilatentattention_pa_t_kernel(tc, x, Wqa, Wqb, out):
                 out=result_tiles[n][:, :, :, 0:PLAIN], in_=plain_banks[n][:].rearrange("p t (h f) -> p t h f", f=PLAIN)
             )
 
-        def rotated_part(n):
-            return result_tiles[n][:, :, :, PLAIN:HEAD_DIM].rearrange("p t h (j e) -> p t h j e", e=2)
-
         def rotate_and_store(n):
-            shape = [P, TILES, HEADS, PAIRS, 2]
-            pairs = rotated_banks[n][:].rearrange("p t (h j e) -> p t h j e", h=HEADS, e=2)
+            step = TILES if n < UNITS - 1 else 1
             first_table = (n % (TABLES // TILES)) * TILES
-            tables = slice(first_table, first_table + TILES)
-            from_w = stage.tile(shape, F32, name="from_w")
-            nc.vector.tensor_tensor(
-                out=rotated_part(n),
-                in0=pairs[:, :, :, :, 0:1].to_broadcast(shape),
-                in1=cos_sin[:, tables].unsqueeze(2).to_broadcast(shape),
-                op=ALU.mult,
-            )
-            nc.vector.tensor_tensor(
-                out=from_w[:],
-                in0=pairs[:, :, :, :, 1:2].to_broadcast(shape),
-                in1=nsin_cos[:, tables].unsqueeze(2).to_broadcast(shape),
-                op=ALU.mult,
-            )
-            nc.gpsimd.tensor_tensor(out=rotated_part(n), in0=rotated_part(n), in1=from_w[:], op=ALU.add)
-            nc.sync.dma_start(out=out_units[n], in_=result_tiles[n][:].rearrange("p t h d -> p (t h d)"))
+            pairs = rotated_banks[n][:].rearrange("p t (h j e) -> p t h j e", h=HEADS, e=2)
+            result = result_tiles[n]
+            from_w = stage.tile([P, TILES, HEADS, PAIRS, 2], F32, name="from_w")
+            for t in range(0, TILES, step):
+                shape = [P, step, HEADS, PAIRS, 2]
+                tiles = slice(t, t + step)
+                tables = slice(first_table + t, first_table + t + step)
+                rotated = result[:, tiles, :, PLAIN:HEAD_DIM].rearrange("p t h (j e) -> p t h j e", e=2)
+                nc.vector.tensor_tensor(
+                    out=rotated,
+                    in0=pairs[:, tiles, :, :, 0:1].to_broadcast(shape),
+                    in1=cos_sin[:, tables].unsqueeze(2).to_broadcast(shape),
+                    op=ALU.mult,
+                )
+                nc.vector.tensor_tensor(
+                    out=from_w[:, tiles],
+                    in0=pairs[:, tiles, :, :, 1:2].to_broadcast(shape),
+                    in1=nsin_cos[:, tables].unsqueeze(2).to_broadcast(shape),
+                    op=ALU.mult,
+                )
+                nc.gpsimd.tensor_tensor(out=rotated, in0=rotated, in1=from_w[:, tiles], op=ALU.add)
+                nc.sync.dma_start(out=out_units[n][:, tiles], in_=result[:, tiles].rearrange("p t h d -> p t (h d)"))
+
+        def vector_copies_plain(n):
+            return n % 2 == 1 and n + ROUND_ROTATE < UNITS
 
         def in_range(n):
             return 0 <= n < UNITS
@@ -251,15 +257,15 @@ def tile_multilatentattention_pa_t_kernel(tc, x, Wqa, Wqb, out):
                 first_product(i - ROUND_FIRST)
             if in_range(i - ROUND_SECOND):
                 second_product(i - ROUND_SECOND)
-                if (i - ROUND_SECOND) % 2 == 0:
+                if not vector_copies_plain(i - ROUND_SECOND):
                     copy_plain(i - ROUND_SECOND, nc.scalar.copy)
             if in_range(i - ROUND_ROTATE):
-                if (i - ROUND_ROTATE) % 2 == 1:
+                if vector_copies_plain(i - ROUND_ROTATE):
                     copy_plain(i - ROUND_ROTATE, nc.vector.tensor_copy)
                 rotate_and_store(i - ROUND_ROTATE)
             if in_range(i):
                 quantise_x(i)
             if in_range(i - ROUND_FIRST):
                 quantise_cq(i - ROUND_FIRST)
-            if i == 0:
+            if i == ROUND_LATE_SETUP:
                 late_setup()

import math
from contextlib import ExitStack

import concourse.masks as masks
import concourse.mybir as mybir

F32 = mybir.dt.float32
BF16 = mybir.dt.bfloat16
I32 = mybir.dt.int32
U32 = mybir.dt.uint32
U8 = mybir.dt.uint8
FP8X4 = mybir.dt.float8_e4m3fn_x4
ALU = mybir.AluOpType
SIN = mybir.ActivationFunctionType.Sin

P = 128
PACK = 4
K_PASS = P * PACK

TOKENS = 4 * 1024
SEQ = 1024
D = 1024
QL = 512
HEADS = 4
HEAD_DIM = 128
PLAIN = 64
PAIRS = 32
BASE = 10000.0

PASSES = D // K_PASS
WORDS = D // 2
TILES = 2
UNIT = TILES * P
UNITS = TOKENS // UNIT
TABLES = SEQ // P
HALF = HEADS * PLAIN

FLOPS = 2 * TOKENS * D * QL + 2 * TOKENS * QL * HEADS * HEAD_DIM

TWO_PI = 2.0 * math.pi

ROUND_FIRST = 2
ROUND_SECOND = 3
ROUND_ROTATE = 4
ROUND_LATE_SETUP = 1

WQA_VECTOR_COLUMNS = 96


def rotation_phases(nc, pool, position_int):
    shape = [P, TABLES, PAIRS, 2]
    turns = pool.tile(shape, F32)
    nc.vector.tensor_scalar(
        out=turns[:, :, 0:1, 1], in0=position_int[:].unsqueeze(2), scalar1=1.0 / TWO_PI, scalar2=None, op0=ALU.mult
    )
    for n in (1, 2, 4, 8, 16):
        nc.vector.tensor_scalar(
            out=turns[:, :, n : 2 * n, 1],
            in0=turns[:, :, 0:n, 1],
            scalar1=BASE ** (-n / PAIRS),
            scalar2=None,
            op0=ALU.mult,
        )
    nc.vector.tensor_scalar(out=turns[:, :, :, 0], in0=turns[:, :, :, 1], scalar1=0.25, scalar2=None, op0=ALU.add)
    whole_int = pool.tile(shape, I32)
    nc.vector.tensor_copy(out=whole_int[:], in_=turns[:])
    whole = pool.tile(shape, F32)
    nc.vector.tensor_copy(out=whole[:], in_=whole_int[:])
    phase = pool.tile(shape, F32)
    nc.vector.tensor_tensor(out=phase[:], in0=turns[:], in1=whole[:], op=ALU.subtract)
    return phase


def tile_multilatentattention_pa_t_kernel(tc, x, Wqa, Wqb, out):
    nc = tc.nc
    x_units = x.flatten_outer_dims().rearrange("(n p t) k -> n p (t k)", p=P, t=TILES)
    out_units = out.rearrange("b s h d -> (b s) (h d)").rearrange("(n p t) f -> n p t f", p=P, t=TILES)

    with ExitStack() as ctx:
        keep = ctx.enter_context(tc.tile_pool(name="keep", bufs=1))
        x_pool = ctx.enter_context(tc.tile_pool(name="x_pool", bufs=UNITS))
        stage = ctx.enter_context(tc.tile_pool(name="stage", bufs=3))
        results = ctx.enter_context(tc.tile_pool(name="results", bufs=4))
        psum = ctx.enter_context(tc.psum_pool(name="psum", bufs=2))
        ctx.enter_context(tc.manual_schedule())

        wa_raw = keep.tile([P, PASSES, PACK, QL], BF16)
        nc.sync.dma_start(
            out=wa_raw[:].rearrange("p g t c -> p (g t c)").rearrange("p (a c) -> p a c", a=2 * PASSES),
            in_=Wqa.rearrange("(a p e) c -> p a (e c)", p=P, e=2),
        )
        wb_raw = keep.tile([P, PACK, HEADS * HEAD_DIM], BF16)
        x_tiles = []
        for n in range(UNITS):
            x_sb = x_pool.tile([P, TILES * D], BF16)
            nc.sync.dma_start(out=x_sb[:], in_=x_units[n])
            x_tiles.append(x_sb)
            if n == ROUND_FIRST:
                nc.sync.dma_start(
                    out=wb_raw[:].rearrange("p j f -> p (j f)"), in_=Wqb.rearrange("(p j) f -> p (j f)", j=PACK)
                )

        position_int = keep.tile([P, TABLES], I32)
        nc.gpsimd.iota(
            position_int[:], pattern=[[UNIT, TABLES // TILES], [1, TILES]], base=0, channel_multiplier=TILES
        )
        identity = keep.tile([P, P], F32)
        masks.make_identity(nc, identity[:])
        phase = rotation_phases(nc, keep, position_int)

        wa_grouped = keep.tile([P, PASSES, QL * PACK], BF16, align_bytes=64)
        wa_codes = keep.tile([P, PASSES, QL], U32, align_bytes=64)
        wa_scales = keep.tile([P, PASSES, QL], U8, align_bytes=64)
        for g in range(PASSES):
            wa_sorted = wa_grouped[:, g].rearrange("p (m i t) -> p m i t", m=PACK, t=PACK)
            wa_rows = wa_raw[:, g].rearrange("p t (i m) -> p m i t", m=PACK)
            nc.vector.tensor_copy(out=wa_sorted[:, :, 0:WQA_VECTOR_COLUMNS], in_=wa_rows[:, :, 0:WQA_VECTOR_COLUMNS])
            nc.scalar.copy(out=wa_sorted[:, :, WQA_VECTOR_COLUMNS:P], in_=wa_rows[:, :, WQA_VECTOR_COLUMNS:P])
        for g in range(PASSES):
            nc.vector.quantize_mx(out=wa_codes[:, g].bitcast(FP8X4), scales=wa_scales[:, g], in_=wa_grouped[:, g])

        cos_sin = keep.tile([P, TABLES, PAIRS, 2], F32)
        nc.scalar.activation(out=cos_sin[:], in_=phase[:], func=SIN, scale=TWO_PI)
        nsin_cos = keep.tile([P, TABLES, PAIRS, 2], F32)
        wb_codes = keep.tile([P, 2 * HALF], U32, align_bytes=64)
        wb_scales = keep.tile([P, 2 * HALF], U8, align_bytes=64)

        def late_setup():
            nc.scalar.mul(out=nsin_cos[:, :, :, 0], in_=cos_sin[:, :, :, 1], mul=-1.0)
            nc.scalar.copy(out=nsin_cos[:, :, :, 1], in_=cos_sin[:, :, :, 0])
            wb_grouped = keep.tile([P, 2, HALF * PACK], BF16, align_bytes=64)
            wb_sorted = wb_raw[:].rearrange("p j (h s f) -> p s h f j", s=2, f=PLAIN)
            for s in range(2):
                nc.vector.tensor_copy(
                    out=wb_grouped[:, s].rearrange("p (h f j) -> p h f j", h=HEADS, j=PACK), in_=wb_sorted[:, s]
                )
            nc.vector.quantize_mx(
                out=wb_codes[:].bitcast(FP8X4), scales=wb_scales[:], in_=wb_grouped[:].rearrange("p s c -> p (s c)")
            )

        x_grouped, x_packed, cq_grouped, cq_packed = {}, {}, {}, {}
        plain_banks, rotated_banks, result_tiles = {}, {}, {}

        def transpose_x(n):
            x_words = x_tiles[n][:].bitcast(F32)
            grouped = stage.tile([P, PASSES * TILES * P * PACK], BF16, align_bytes=64, name="x_grouped")
            grouped_words = grouped[:].bitcast(F32).rearrange("p (g t r u) -> p g t r u", g=PASSES, t=TILES, u=2)
            for t in range(TILES):
                x_t = psum.tile([P, 2 * PASSES, P], F32, name="x_t")
                for a in range(2 * PASSES):
                    first_word = t * WORDS + a * P
                    nc.tensor.transpose(x_t[:, a, :], x_words[:, first_word : first_word + P], identity[:])
                nc.scalar.copy(out=grouped_words[:, :, t], in_=x_t[:].rearrange("p (g u) r -> p g r u", u=2))
            x_grouped[n] = grouped

        def quantise_x(n):
            codes = stage.tile([P, PASSES, TILES, P], U32, align_bytes=64, name="x_codes")
            scales = stage.tile([P, PASSES, TILES, P], U8, align_bytes=64, name="x_scales")
            nc.vector.quantize_mx(
                out=codes[:].rearrange("p g t r -> p (g t r)").bitcast(FP8X4),
                scales=scales[:].rearrange("p g t r -> p (g t r)"),
                in_=x_grouped[n][:],
            )
            x_packed[n] = (codes, scales)

        def first_product(n):
            codes, scales = x_packed[n]
            grouped = stage.tile([P, TILES, P, PACK], BF16, align_bytes=64, name="cq_grouped")
            for t in range(TILES):
                cq_t = psum.tile([P, PACK, P], F32, name="cq_t")
                for m in range(PACK):
                    columns = slice(m * P, (m + 1) * P)
                    for g in range(PASSES):
                        nc.tensor.matmul_mx(
                            out=cq_t[:, m, :],
                            lhsT=wa_codes[:, g, columns].bitcast(FP8X4),
                            lhsT_scale=wa_scales[:, g, columns],
                            rhs=codes[:, g, t, :].bitcast(FP8X4),
                            rhs_scale=scales[:, g, t, :],
                            start=(g == 0),
                            stop=(g == PASSES - 1),
                        )
                nc.scalar.copy(out=grouped[:, t], in_=cq_t[:].rearrange("p m r -> p r m"))
            cq_grouped[n] = grouped

        def quantise_cq(n):
            codes = stage.tile([P, TILES, P], U32, align_bytes=64, name="cq_codes")
            scales = stage.tile([P, TILES, P], U8, align_bytes=64, name="cq_scales")
            nc.vector.quantize_mx(
                out=codes[:].rearrange("p t r -> p (t r)").bitcast(FP8X4),
                scales=scales[:].rearrange("p t r -> p (t r)"),
                in_=cq_grouped[n][:].rearrange("p t r m -> p (t r m)"),
            )
            cq_packed[n] = (codes, scales)

        def second_product(n):
            codes, scales = cq_packed[n]
            plain_bank = psum.tile([P, TILES, HALF], F32, name="plain_bank")
            rotated_bank = psum.tile([P, TILES, HALF], F32, name="rotated_bank")
            for t in range(TILES):
                for s, bank in enumerate((plain_bank, rotated_bank)):
                    columns = slice(s * HALF, (s + 1) * HALF)
                    nc.tensor.matmul_mx(
                        out=bank[:, t, :],
                        lhsT=codes[:, t, :].bitcast(FP8X4),
                        lhsT_scale=scales[:, t, :],
                        rhs=wb_codes[:, columns].bitcast(FP8X4),
                        rhs_scale=wb_scales[:, columns],
                        start=True,
                        stop=True,
                    )
            plain_banks[n] = plain_bank
            rotated_banks[n] = rotated_bank
            result_tiles[n] = results.tile([P, TILES, HEADS, HEAD_DIM], F32, name="result")

        def copy_plain(n, engine_copy):
            engine_copy(
                out=result_tiles[n][:, :, :, 0:PLAIN], in_=plain_banks[n][:].rearrange("p t (h f) -> p t h f", f=PLAIN)
            )

        def rotate_and_store(n):
            step = TILES if n < UNITS - 1 else 1
            first_table = (n % (TABLES // TILES)) * TILES
            pairs = rotated_banks[n][:].rearrange("p t (h j e) -> p t h j e", h=HEADS, e=2)
            result = result_tiles[n]
            from_w = stage.tile([P, TILES, HEADS, PAIRS, 2], F32, name="from_w")
            for t in range(0, TILES, step):
                shape = [P, step, HEADS, PAIRS, 2]
                tiles = slice(t, t + step)
                tables = slice(first_table + t, first_table + t + step)
                rotated = result[:, tiles, :, PLAIN:HEAD_DIM].rearrange("p t h (j e) -> p t h j e", e=2)
                nc.vector.tensor_tensor(
                    out=rotated,
                    in0=pairs[:, tiles, :, :, 0:1].to_broadcast(shape),
                    in1=cos_sin[:, tables].unsqueeze(2).to_broadcast(shape),
                    op=ALU.mult,
                )
                nc.vector.tensor_tensor(
                    out=from_w[:, tiles],
                    in0=pairs[:, tiles, :, :, 1:2].to_broadcast(shape),
                    in1=nsin_cos[:, tables].unsqueeze(2).to_broadcast(shape),
                    op=ALU.mult,
                )
                nc.gpsimd.tensor_tensor(out=rotated, in0=rotated, in1=from_w[:, tiles], op=ALU.add)
                nc.sync.dma_start(out=out_units[n][:, tiles], in_=result[:, tiles].rearrange("p t h d -> p t (h d)"))

        def vector_copies_plain(n):
            return n % 2 == 1 and n + ROUND_ROTATE < UNITS

        def in_range(n):
            return 0 <= n < UNITS

        for i in range(UNITS + ROUND_ROTATE):
            if in_range(i):
                transpose_x(i)
            if in_range(i - ROUND_FIRST):
                first_product(i - ROUND_FIRST)
            if in_range(i - ROUND_SECOND):
                second_product(i - ROUND_SECOND)
                if not vector_copies_plain(i - ROUND_SECOND):
                    copy_plain(i - ROUND_SECOND, nc.scalar.copy)
            if in_range(i - ROUND_ROTATE):
                if vector_copies_plain(i - ROUND_ROTATE):
                    copy_plain(i - ROUND_ROTATE, nc.vector.tensor_copy)
                rotate_and_store(i - ROUND_ROTATE)
            if in_range(i):
                quantise_x(i)
            if in_range(i - ROUND_FIRST):
                quantise_cq(i - ROUND_FIRST)
            if i == ROUND_LATE_SETUP:
                late_setup()
